import numpy as np
import ml_dtypes


def mxq(x, axis, fmt="e4m3"):
    dtype, down = {"e4m3": (ml_dtypes.float8_e4m3fn, 7), "e5m2": (ml_dtypes.float8_e5m2, 14)}[fmt]
    v = np.moveaxis(np.asarray(x, np.float32).astype(ml_dtypes.bfloat16).astype(np.float64), axis, -1)
    blocks = v.reshape(v.shape[:-1] + (-1, 32))
    amax = np.abs(blocks).max(-1, keepdims=True)
    byte = np.maximum(np.where(amax > 0, np.frexp(amax)[1] - 1 + 127, 0) - down, 1)
    scale = np.exp2(byte - 127.0)
    codes = (blocks / scale).astype(np.float32).astype(dtype).astype(np.float64)
    return np.moveaxis((codes * scale).reshape(v.shape), -1, axis)


WIDE = False


def mx_kscale(k):
    if not WIDE:
        return np.ones(k)
    levels = np.array([10, -10, 5, -5, 0])
    if k % 512:
        return np.exp2(np.random.permutation(np.resize(levels, k // 32))).repeat(32)
    a = np.empty((k // 512, 16))
    for p in range(k // 512):
        a[p, :8] = np.random.permutation(np.resize(levels, 8))
        for g in range(8):
            far = levels[np.abs(levels - a[p, g]) >= 10]
            a[p, g + 8] = far[np.random.randint(len(far))]
    return np.exp2(a.ravel()).repeat(32)


BF16 = ml_dtypes.bfloat16


def bf(x):
    return np.asarray(x, np.float32).astype(BF16)


def f64(x):
    return np.asarray(x).astype(np.float64)


E2M1 = np.array([0.0, 0.5, 1.0, 1.5, 2.0, 3.0, 4.0, 6.0, -0.0, -0.5, -1.0, -1.5, -2.0, -3.0, -4.0, -6.0])


def pack_weight(w, fmt):
    k, n = w.shape
    w = f64(bf(w)).reshape(k // 32, 32, n)
    amax = np.abs(w).max(1)
    if fmt == "e4m3":
        byte = np.frexp(amax)[1] - 1 + 127 - 7
    else:
        mant, ex = np.frexp(amax / 6.0)
        byte = np.where(mant > 0.5, ex, ex - 1) + 127
    byte = np.clip(np.where(amax > 0, byte, 1), 1, 254)
    scaled = (w * np.exp2(127.0 - byte)[:, None, :]).reshape(k, n).astype(np.float32)
    by_word = np.ascontiguousarray(scaled.reshape(k // 512, 128, 4, n).transpose(0, 1, 3, 2))
    if fmt == "e4m3":
        words = by_word.astype(ml_dtypes.float8_e4m3fn).view(np.uint8)
    else:
        c = by_word.astype(ml_dtypes.float4_e2m1fn).view(np.uint8) & 0xF
        words = c[..., 0::2] | (c[..., 1::2] << 4)
    return np.ascontiguousarray(words), np.ascontiguousarray(byte.astype(np.uint8).reshape(k // 512, 16, n))


def unpack_weight(words, scales, fmt):
    g, p, n, _ = words.shape
    if fmt == "e4m3":
        vals = np.ascontiguousarray(words).view(ml_dtypes.float8_e4m3fn).astype(np.float64)
    else:
        nib = np.empty((g, p, n, 4), np.uint8)
        nib[..., 0::2] = words & 0xF
        nib[..., 1::2] = words >> 4
        vals = E2M1[nib]
    vals = vals * np.repeat(np.exp2(scales.astype(np.float64) - 127.0), 8, axis=1)[..., None]
    return vals.transpose(0, 1, 3, 2).reshape(g * 512, n)
def pack4(w):
    words, scales = pack_weight(w, "e2m1")
    return words.reshape(words.shape[0], 128, -1), scales


def unpack4(words, scales):
    return unpack_weight(words.reshape(words.shape[0], 128, -1, 2), scales, "e2m1")


B, T, D, E, F = 4, 1024, 512, 1024, 256
EPS = 1e-6


def rms_norm(x, w):
    rms = np.sqrt(np.mean(x * x, axis=-1, keepdims=True) + EPS)
    return x / rms * w


def erf(v):
    a = np.minimum(np.abs(v), 6.0)
    z = 2.0 * a * a
    term = a.copy()
    tot = a.copy()
    for n in range(1, 110):
        term = term * z / (2 * n + 1)
        tot = tot + term
    return np.sign(v) * tot * np.exp(-a * a) * 2.0 / np.sqrt(np.pi)


def gelu_erf(v):
    return 0.5 * v * (1.0 + erf(v / np.sqrt(2.0)))


def draw0():
    s, t = mx_kscale(E), mx_kscale(D)
    attn = bf(np.random.standard_normal((B, T, E)) * 0.6 * s)
    x = bf(np.random.standard_normal((B, T, D)))
    wo_words, wo_scales = pack4(np.random.standard_normal((E, D)) / np.sqrt(E) / s[:, None])
    bo = bf(np.random.standard_normal(D) * 0.1)
    mlp_norm_w = bf((1.0 + 0.1 * np.random.standard_normal(D)) * t)
    w1_words, w1_scales = pack4(np.random.standard_normal((D, F)) / np.sqrt(D) / t[:, None])
    b1 = bf(np.random.standard_normal(F) * 0.1)
    return {"attn": attn,
            "x": x,
            "wo_words": wo_words,
            "wo_scales": wo_scales,
            "bo": bo,
            "mlp_norm_w": mlp_norm_w,
            "w1_words": w1_words,
            "w1_scales": w1_scales,
            "b1": b1}


def core(attn, x, wo_words, wo_scales, bo, mlp_norm_w, w1_words, w1_scales, b1):
    x_mid = f64(x) + (mxq(f64(attn), 2, "e4m3") @ unpack4(wo_words, wo_scales)) + f64(bo)
    h = rms_norm(x_mid, f64(mlp_norm_w))
    g = gelu_erf((mxq(h, 2, "e4m3") @ unpack4(w1_words, w1_scales)) + f64(b1))
    return x_mid, g


def e4m3fn_bytes(y):
    return np.clip(np.asarray(y, np.float64), -448.0, 448.0).astype(np.float32).astype(ml_dtypes.float8_e4m3fn).view(np.uint8)


def e4m3fn_values(b):
    return np.asarray(b, np.uint8).view(ml_dtypes.float8_e4m3fn).astype(np.float64)


def setup_inputs():
    d = draw0()
    x0 = np.asarray(d['attn']).astype(np.float64)
    s = (np.max(np.abs(x0), axis=(0, 1), keepdims=True) / 448.0).astype(np.float32)
    out = {}
    for k, v in d.items():
        if k == 'attn':
            out['attn_bytes'] = e4m3fn_bytes(x0 / s.astype(np.float64))
            out['attn_scale'] = s
        else:
            out[k] = v
    return out


def reference(attn_bytes, attn_scale, x, wo_words, wo_scales, bo, mlp_norm_w, w1_words, w1_scales, b1):
    return core(e4m3fn_values(attn_bytes) * attn_scale.astype(np.float64), x, wo_words, wo_scales, bo, mlp_norm_w, w1_words, w1_scales, b1)

@@ -1,0 +1,272 @@
+from contextlib import ExitStack
+
+import concourse.mybir as mybir
+from concourse.masks import make_identity
+
+F32 = mybir.dt.float32
+BF16 = mybir.dt.bfloat16
+I32 = mybir.dt.int32
+U32 = mybir.dt.uint32
+U8 = mybir.dt.uint8
+FP8 = mybir.dt.float8_e4m3fn
+FP8X4 = mybir.dt.float8_e4m3fn_x4
+FP4X4 = mybir.dt.float4_e2m1fn_x4
+ACT = mybir.ActivationFunctionType
+ALU = mybir.AluOpType
+
+TOKENS, E, D, F = 4096, 1024, 512, 256
+EPS = 1e-6
+P = 128
+TILES = TOKENS // P
+PAIRS = TILES // 2
+FLOPS = 2 * TOKENS * E * D + 2 * TOKENS * D * F
+
+
+def tile_tinyblock_pb_t_w4_kernel(tc, attn_bytes, attn_scale, x, wo_words, wo_scales, bo, mlp_norm_w, w1_words, w1_scales, b1, out_0, out_1):
+    nc = tc.nc
+    bytes_v = attn_bytes.flatten_outer_dims().rearrange("(p j) k -> p j k", j=TILES)
+    x_v = x.flatten_outer_dims().rearrange("(p j) d -> p j d", j=TILES)
+    mid_v = out_0.flatten_outer_dims().rearrange("(p j) d -> p j d", j=TILES)
+    g_v = out_1.flatten_outer_dims().rearrange("(p j) f -> p j f", j=TILES)
+
+    with ExitStack() as ctx:
+        const = ctx.enter_context(tc.tile_pool(name="const", bufs=1))
+        keep = ctx.enter_context(tc.tile_pool(name="keep", bufs=PAIRS))
+        work = ctx.enter_context(tc.tile_pool(name="work", bufs=2))
+        deep = ctx.enter_context(tc.tile_pool(name="deep", bufs=5))
+        ps2 = ctx.enter_context(tc.psum_pool(name="ps2", bufs=2))
+        ps1 = ctx.enter_context(tc.psum_pool(name="ps1", bufs=1))
+        ctx.enter_context(tc.manual_schedule())
+
+        warm = const.tile([P, 1], F32, name="warm")
+        nc.vector.memset(warm[:], 0.0)
+        warm_out = const.tile([P, 1], F32, name="warm_out")
+        nc.scalar.activation(out=warm_out[:], in_=warm[:], func=ACT.Gelu)
+        ident = const.tile([P, P], F32, name="ident")
+        make_identity(nc, ident[:])
+        wplanes = const.tile([P, 2 * D + F], U8, name="wplanes", align_bytes=64)
+        nc.vector.memset(wplanes[:].bitcast(I32), 0)
+        rows = const.tile([P, 2 * D + F], BF16, name="rows")
+        nc.vector.memset(rows[:], 0.0)
+        ones = const.tile([P, P], BF16, name="ones")
+        nc.vector.memset(ones[:], 1.0)
+        half = const.tile([P, 2], F32, name="half")
+        nc.vector.memset(half[:], -0.5)
+
+        abytes = []
+        xin = []
+        for n in range(PAIRS):
+            abytes_t = keep.tile([P, 2, E], U8, name="abytes")
+            xin_t = keep.tile([P, 2, D], BF16, name="xin")
+            abytes.append(abytes_t)
+            xin.append(xin_t)
+
+        def load_bytes(n):
+            nc.sync.dma_start(out=abytes[n][:], in_=bytes_v[:, 2 * n : 2 * n + 2, :])
+
+        def load_x(n):
+            nc.sync.dma_start(out=xin[n][:], in_=x_v[:, 2 * n : 2 * n + 2, :])
+
+        for j in range(2):
+            nc.sync.dma_start(out=abytes[0][:, j, :], in_=bytes_v[:, j, :])
+        ascale = const.tile([P, 2, 2, 2], F32, name="ascale")
+        nc.sync.dma_start(out=ascale[:].rearrange("p g u e -> p g (u e)"), in_=attn_scale.rearrange("a b (g p t) -> p (a b g) t", p=P, t=4))
+        wo_t = const.tile([P, 4 * D], U8, name="wo_t", align_bytes=64)
+        nc.sync.dma_start(out=wo_t[:].bitcast(I32).rearrange("p (g w) -> p g w", g=2), in_=wo_words.bitcast(I32).rearrange("g p w -> p g w"))
+        for q in range(4):
+            nc.sync.dma_start(out=wplanes[32 * q : 32 * q + 4, 0 : 2 * D].bitcast(I32).rearrange("q (g n) -> q g n", g=2), in_=wo_scales[:, 4 * q : 4 * q + 4, :].bitcast(I32).rearrange("g q n -> q g n"))
+        for q in range(4):
+            nc.sync.dma_start(out=wplanes[32 * q : 32 * q + 4, 2 * D : 2 * D + F].bitcast(I32), in_=w1_scales[0, 4 * q : 4 * q + 4, :].bitcast(I32))
+        nc.sync.dma_start(out=rows[0:1, 0:D], in_=bo.unsqueeze(0))
+        nc.sync.dma_start(out=rows[0:1, D : 2 * D], in_=mlp_norm_w.unsqueeze(0))
+        nc.sync.dma_start(out=rows[0:1, 2 * D : 2 * D + F], in_=b1.unsqueeze(0))
+        w1_t = const.tile([P, 2 * F], U8, name="w1_t", align_bytes=64)
+        nc.sync.dma_start(out=w1_t[:].bitcast(I32), in_=w1_words[0].bitcast(I32))
+        load_x(0)
+        load_bytes(1)
+        load_x(1)
+        for n in range(2, PAIRS):
+            load_bytes(n)
+            load_x(n)
+
+        gain = ps1.tile([P, D], F32, name="gain")
+        bo_b = const.tile([P, D], BF16, name="bo_b")
+        b1_col = const.tile([P, 2], F32, name="b1_col")
+
+        def vectors():
+            nc.tensor.matmul(gain[:], lhsT=ones[:], rhs=rows[:, D : 2 * D], start=True, stop=True)
+            spread = ps2.tile([P, D], F32, name="acc")
+            nc.tensor.matmul(spread[:], lhsT=ones[:], rhs=rows[:, 0:D], start=True, stop=True)
+            nc.scalar.copy(out=bo_b[:], in_=spread[:])
+            col = ps1.tile([P, 2, F], F32, name="mx2")
+            for c in range(2):
+                nc.tensor.matmul(col[:, c, 0:8], lhsT=rows[:, 2 * D + P * c : 2 * D + P * (c + 1)], rhs=ones[:, 0:8], start=True, stop=True)
+            nc.vector.tensor_copy(out=b1_col[:], in_=col[:, :, 0])
+
+        a16, t1, codes, planes, acc, xb, xm, ss, rstd = {}, {}, {}, {}, {}, {}, {}, {}, {}
+        grouped, h, t2, h4, hcodes, hplanes, mx2, gt, t3 = {}, {}, {}, {}, {}, {}, {}, {}, {}
+
+        def cast(n):
+            a16_t = work.tile([P, 2, E], BF16, name="a16", bufs=3)
+            a16[n] = a16_t
+            if n == 0:
+                for j in range(2):
+                    nc.scalar.copy(out=a16_t[:, j, :], in_=abytes[n][:, j, :].bitcast(FP8))
+            else:
+                nc.scalar.copy(out=a16_t[:], in_=abytes[n][:].bitcast(FP8))
+
+        def turn_attn(n):
+            for j in range(2):
+                bank = ps2.tile([P, 2, 2, P], F32, name="t1")
+                t1[n, j] = bank
+                words = a16[n][:, j, :].bitcast(F32)
+                for g in range(2):
+                    for u in range(2):
+                        nc.tensor.transpose(bank[:, g, u, :], words[:, 256 * g + u : 256 * (g + 1) : 2], ident[:])
+
+        def scale_attn(n):
+            grouped_t = work.tile([P, 2, 2, P, 4], BF16, name="grouped", align_bytes=64)
+            grouped[n] = grouped_t
+            for j in range(2):
+                pairs = t1[n, j][:].rearrange("p g u r -> p (g u r)").bitcast(BF16).rearrange("p (g u r e) -> p g u r e", g=2, u=2, e=2)
+                for g in range(2):
+                    nc.vector.tensor_tensor(
+                        out=grouped_t[:, j, g].rearrange("p r (u e) -> p r u e", u=2),
+                        in0=pairs[:, g].rearrange("p u r e -> p r u e"),
+                        in1=ascale[:, g].unsqueeze(1).to_broadcast([P, P, 2, 2]),
+                        op=ALU.mult,
+                    )
+
+        def quant_attn(n):
+            codes_t = work.tile([P, 4 * P], U32, name="codes", align_bytes=64)
+            planes_t = work.tile([P, 4 * P], U8, name="planes", align_bytes=64)
+            codes[n], planes[n] = codes_t, planes_t
+            nc.vector.quantize_mx(out=codes_t[:].bitcast(FP8X4), scales=planes_t[:], in_=grouped[n][:].rearrange("p j g r t -> p (j g r t)"))
+
+        def project(n):
+            for j in range(2):
+                acc_t = ps2.tile([P, D], F32, name="acc")
+                acc[n, j] = acc_t
+                for g in range(2):
+                    cols = slice((2 * j + g) * P, (2 * j + g + 1) * P)
+                    nc.tensor.matmul_mx(
+                        out=acc_t[:],
+                        lhsT=codes[n][:, cols].bitcast(FP8X4),
+                        lhsT_scale=planes[n][:, cols],
+                        rhs=wo_t[:, 2 * D * g : 2 * D * (g + 1)].bitcast(FP4X4),
+                        rhs_scale=wplanes[:, D * g : D * (g + 1)],
+                        start=(g == 0),
+                        stop=(g == 1),
+                    )
+
+        def add_bo(n):
+            xb_t = work.tile([P, 2, D], F32, name="xb", bufs=3)
+            xb[n] = xb_t
+            for j in range(2):
+                nc.gpsimd.tensor_tensor(out=xb_t[:, j, :], in0=xin[n][:, j, :], in1=bo_b[:], op=ALU.add)
+
+        def residual(n):
+            xm_t = deep.tile([P, 2, D], F32, name="xm")
+            xm[n] = xm_t
+            for j in range(2):
+                nc.vector.tensor_tensor(out=xm_t[:, j, :], in0=acc[n, j][:], in1=xb[n][:, j, :], op=ALU.add)
+            nc.sync.dma_start(out=mid_v[:, 2 * n : 2 * n + 2, :], in_=xm_t[:])
+
+        def squares(n):
+            ss_t = work.tile([P, 2], F32, name="ss")
+            ss[n] = ss_t
+            for j in range(2):
+                junk = work.tile([P, D], BF16, name="junk")
+                nc.scalar.activation(out=junk[:], in_=xm[n][:, j, :], func=ACT.Square, accum_out=ss_t[:, j : j + 1])
+
+        def root(n):
+            ms_t = work.tile([P, 2], F32, name="ms")
+            rstd_t = work.tile([P, 2], F32, name="rstd")
+            rstd[n] = rstd_t
+            nc.gpsimd.tensor_scalar(out=ms_t[:], in0=ss[n][:], scalar1=1.0 / D, scalar2=EPS, op0=ALU.mult, op1=ALU.add)
+            nc.gpsimd.tensor_tensor(out=rstd_t[:], in0=ms_t[:], in1=half[:], op=ALU.pow)
+
+        def norm(n):
+            h_t = work.tile([P, 2, D], BF16, name="h")
+            h[n] = h_t
+            for j in range(2):
+                nc.vector.scalar_tensor_tensor(out=h_t[:, j, :], in0=xm[n][:, j, :], scalar=rstd[n][:, j : j + 1], in1=gain[:], op0=ALU.mult, op1=ALU.mult)
+
+        def turn_h(n):
+            bank = ps1.tile([P, 2, 2, P], F32, name="t2")
+            t2[n] = bank
+            for j in range(2):
+                words = h[n][:, j, :].bitcast(F32)
+                for u in range(2):
+                    nc.tensor.transpose(bank[:, j, u, :], words[:, u:256:2], ident[:])
+
+        def group_h(n):
+            h4_t = work.tile([P, 2, P, 4], BF16, name="h4", align_bytes=64)
+            h4[n] = h4_t
+            nc.scalar.copy(out=h4_t[:].rearrange("p j r t -> p (j r t)").bitcast(F32).rearrange("p (j r u) -> p j r u", j=2, u=2), in_=t2[n][:].rearrange("p j u r -> p j r u"))
+
+        def quant_h(n):
+            hcodes_t = work.tile([P, 2 * P], U32, name="hcodes", align_bytes=64)
+            hplanes_t = work.tile([P, 2 * P], U8, name="hplanes", align_bytes=64)
+            hcodes[n], hplanes[n] = hcodes_t, hplanes_t
+            nc.vector.quantize_mx(out=hcodes_t[:].bitcast(FP8X4), scales=hplanes_t[:], in_=h4[n][:].rearrange("p j r t -> p (j r t)"))
+
+        def expand(n):
+            bank = ps1.tile([P, 2, 2 * P], F32, name="mx2")
+            mx2[n] = bank
+            for c in range(2):
+                nc.tensor.matmul_mx(
+                    out=bank[:, c, :],
+                    lhsT=w1_t[:, 2 * P * c : 2 * P * (c + 1)].bitcast(FP4X4),
+                    lhsT_scale=wplanes[:, 2 * D + P * c : 2 * D + P * (c + 1)],
+                    rhs=hcodes[n][:].bitcast(FP8X4),
+                    rhs_scale=hplanes[n][:],
+                    start=True,
+                    stop=True,
+                )
+
+        def gelu(n):
+            gt_t = work.tile([P, 2, 2 * P], F32, name="gt")
+            gt[n] = gt_t
+            for c in range(2):
+                nc.scalar.activation(out=gt_t[:, c, :], in_=mx2[n][:, c, :], func=ACT.Gelu, bias=b1_col[:, c : c + 1])
+
+        def turn_g(n):
+            bank = ps1.tile([P, 2, 2, P], F32, name="t3")
+            t3[n] = bank
+            for j in range(2):
+                for c in range(2):
+                    nc.tensor.transpose(bank[:, j, c, :], gt[n][:, c, P * j : P * (j + 1)], ident[:])
+
+        def store_g(n):
+            g_t = work.tile([P, 2, F], F32, name="g", bufs=3)
+            nc.scalar.copy(out=g_t[:].rearrange("p j f -> p (j f)"), in_=t3[n][:].rearrange("p j c r -> p (j c r)"))
+            nc.sync.dma_start(out=g_v[:, 2 * n : 2 * n + 2, :], in_=g_t[:])
+
+        def run(stage, n):
+            if 0 <= n < PAIRS:
+                stage(n)
+
+        cast(0)
+        turn_attn(0)
+        cast(1)
+        vectors()
+        add_bo(0)
+        for n in range(PAIRS + 4):
+            run(scale_attn, n)
+            run(gelu, n - 4)
+            run(cast, n + 2)
+            run(turn_h, n - 3)
+            run(turn_g, n - 4)
+            run(turn_attn, n + 1)
+            run(group_h, n - 3)
+            run(store_g, n - 4)
+            run(residual, n - 1)
+            run(squares, n - 1)
+            run(add_bo, n + 1)
+            run(root, n - 1)
+            run(quant_h, n - 3)
+            run(quant_attn, n)
+            run(expand, n - 3)
+            run(project, n)
+            run(norm, n - 2)

@@ -18,7 +18,28 @@ TOKENS, E, D, F = 4096, 1024, 512, 256
 EPS = 1e-6
 P = 128
 TILES = TOKENS // P
-PAIRS = TILES // 2
+GROUPS = [[0], [1]] + [[t, t + 1] for t in range(2, TILES - 2, 2)] + [[TILES - 2], [TILES - 1]]
+ON_GPSIMD = (7, 12, 17, 22, 27)
+STEPS = [
+    ("gpsimd_scale", 1),
+    ("scale_attn", 0),
+    ("residual", -1),
+    ("cast", 2),
+    ("gelu", -4),
+    ("turn_h", -3),
+    ("turn_g", -4),
+    ("turn_attn", 1),
+    ("group_h", -3),
+    ("squares", -1),
+    ("add_bo", 0),
+    ("store_g", -4),
+    ("root", -1),
+    ("quant_h", -3),
+    ("quant_attn", 0),
+    ("expand", -3),
+    ("project", 0),
+    ("norm", -2),
+]
 FLOPS = 2 * TOKENS * E * D + 2 * TOKENS * D * F
 
 
@@ -31,7 +52,7 @@ def tile_tinyblock_pb_t_w4_kernel(tc, attn_bytes, attn_scale, x, wo_words, wo_sc
 
     with ExitStack() as ctx:
         const = ctx.enter_context(tc.tile_pool(name="const", bufs=1))
-        keep = ctx.enter_context(tc.tile_pool(name="keep", bufs=PAIRS))
+        keep = ctx.enter_context(tc.tile_pool(name="keep", bufs=len(GROUPS)))
         work = ctx.enter_context(tc.tile_pool(name="work", bufs=2))
         deep = ctx.enter_context(tc.tile_pool(name="deep", bufs=5))
         ps2 = ctx.enter_context(tc.psum_pool(name="ps2", bufs=2))
@@ -55,22 +76,26 @@ def tile_tinyblock_pb_t_w4_kernel(tc, attn_bytes, attn_scale, x, wo_words, wo_sc
 
         abytes = []
         xin = []
-        for n in range(PAIRS):
+        for tiles in GROUPS:
             abytes_t = keep.tile([P, 2, E], U8, name="abytes")
             xin_t = keep.tile([P, 2, D], BF16, name="xin")
             abytes.append(abytes_t)
             xin.append(xin_t)
 
         def load_bytes(n):
-            nc.sync.dma_start(out=abytes[n][:], in_=bytes_v[:, 2 * n : 2 * n + 2, :])
+            k = len(GROUPS[n])
+            t = GROUPS[n][0]
+            nc.sync.dma_start(out=abytes[n][:, 0:k, :], in_=bytes_v[:, t : t + k, :])
 
         def load_x(n):
-            nc.sync.dma_start(out=xin[n][:], in_=x_v[:, 2 * n : 2 * n + 2, :])
+            k = len(GROUPS[n])
+            t = GROUPS[n][0]
+            nc.sync.dma_start(out=xin[n][:, 0:k, :], in_=x_v[:, t : t + k, :])
 
-        for j in range(2):
-            nc.sync.dma_start(out=abytes[0][:, j, :], in_=bytes_v[:, j, :])
-        ascale = const.tile([P, 2, 2, 2], F32, name="ascale")
-        nc.sync.dma_start(out=ascale[:].rearrange("p g u e -> p g (u e)"), in_=attn_scale.rearrange("a b (g p t) -> p (a b g) t", p=P, t=4))
+        load_bytes(0)
+        load_bytes(1)
+        ascale = const.tile([P, 2, 4], F32, name="ascale")
+        nc.sync.dma_start(out=ascale[:], in_=attn_scale.rearrange("a b (g p t) -> p (a b g) t", p=P, t=4))
         wo_t = const.tile([P, 4 * D], U8, name="wo_t", align_bytes=64)
         nc.sync.dma_start(out=wo_t[:].bitcast(I32).rearrange("p (g w) -> p g w", g=2), in_=wo_words.bitcast(I32).rearrange("g p w -> p g w"))
         for q in range(4):
@@ -83,12 +108,19 @@ def tile_tinyblock_pb_t_w4_kernel(tc, attn_bytes, attn_scale, x, wo_words, wo_sc
         w1_t = const.tile([P, 2 * F], U8, name="w1_t", align_bytes=64)
         nc.sync.dma_start(out=w1_t[:].bitcast(I32), in_=w1_words[0].bitcast(I32))
         load_x(0)
-        load_bytes(1)
+        load_bytes(2)
         load_x(1)
-        for n in range(2, PAIRS):
+        load_bytes(3)
+        load_x(2)
+        ascale_row = const.tile([P, E], F32, name="ascale_row")
+        nc.sync.dma_start(out=ascale_row[:], in_=attn_scale.rearrange("a b k -> (a b k)").partition_broadcast(P))
+        load_x(3)
+        for n in range(4, len(GROUPS)):
             load_bytes(n)
             load_x(n)
 
+        ascale_full = const.tile([P, 2, P, 4], F32, name="ascale_full")
+        nc.vector.tensor_copy(out=ascale_full[:], in_=ascale[:].unsqueeze(2).to_broadcast([P, 2, P, 4]))
         gain = ps1.tile([P, D], F32, name="gain")
         bo_b = const.tile([P, D], BF16, name="bo_b")
         b1_col = const.tile([P, 2], F32, name="b1_col")
@@ -101,50 +133,60 @@ def tile_tinyblock_pb_t_w4_kernel(tc, attn_bytes, attn_scale, x, wo_words, wo_sc
             col = ps1.tile([P, 2, F], F32, name="mx2")
             for c in range(2):
                 nc.tensor.matmul(col[:, c, 0:8], lhsT=rows[:, 2 * D + P * c : 2 * D + P * (c + 1)], rhs=ones[:, 0:8], start=True, stop=True)
-            nc.vector.tensor_copy(out=b1_col[:], in_=col[:, :, 0])
+            nc.scalar.copy(out=b1_col[:], in_=col[:, :, 0])
 
         a16, t1, codes, planes, acc, xb, xm, ss, rstd = {}, {}, {}, {}, {}, {}, {}, {}, {}
         grouped, h, t2, h4, hcodes, hplanes, mx2, gt, t3 = {}, {}, {}, {}, {}, {}, {}, {}, {}
+        scaled = {}
 
-        def cast(n):
+        def cast(n, k):
             a16_t = work.tile([P, 2, E], BF16, name="a16", bufs=3)
             a16[n] = a16_t
-            if n == 0:
-                for j in range(2):
-                    nc.scalar.copy(out=a16_t[:, j, :], in_=abytes[n][:, j, :].bitcast(FP8))
-            else:
-                nc.scalar.copy(out=a16_t[:], in_=abytes[n][:].bitcast(FP8))
+            nc.scalar.copy(out=a16_t[:, 0:k, :], in_=abytes[n][:, 0:k, :].bitcast(FP8))
 
-        def turn_attn(n):
-            for j in range(2):
+        def gpsimd_scale(n, k):
+            for j, t in enumerate(GROUPS[n]):
+                if t in ON_GPSIMD:
+                    scaled_t = work.tile([P, E], BF16, name="scaled")
+                    scaled[t] = scaled_t
+                    nc.gpsimd.tensor_tensor(out=scaled_t[:], in0=a16[n][:, j, :], in1=ascale_row[:], op=ALU.mult)
+
+        def turn_attn(n, k):
+            for j, t in enumerate(GROUPS[n]):
                 bank = ps2.tile([P, 2, 2, P], F32, name="t1")
                 t1[n, j] = bank
-                words = a16[n][:, j, :].bitcast(F32)
+                source = scaled[t][:] if t in ON_GPSIMD else a16[n][:, j, :]
+                words = source.bitcast(F32)
                 for g in range(2):
                     for u in range(2):
-                        nc.tensor.transpose(bank[:, g, u, :], words[:, 256 * g + u : 256 * (g + 1) : 2], ident[:])
+                        nc.tensor.transpose(bank[:, u, g, :], words[:, 256 * g + u : 256 * (g + 1) : 2], ident[:])
 
-        def scale_attn(n):
+        def scale_attn(n, k):
             grouped_t = work.tile([P, 2, 2, P, 4], BF16, name="grouped", align_bytes=64)
             grouped[n] = grouped_t
-            for j in range(2):
-                pairs = t1[n, j][:].rearrange("p g u r -> p (g u r)").bitcast(BF16).rearrange("p (g u r e) -> p g u r e", g=2, u=2, e=2)
-                for g in range(2):
+            for j in reversed(range(k)):
+                if GROUPS[n][j] in ON_GPSIMD:
+                    nc.scalar.copy(
+                        out=grouped_t[:, j].rearrange("p g r t -> p (g r t)").bitcast(F32).rearrange("p (q u) -> p q u", u=2),
+                        in_=t1[n, j][:].rearrange("p u g r -> p (g r) u"),
+                    )
+                else:
                     nc.vector.tensor_tensor(
-                        out=grouped_t[:, j, g].rearrange("p r (u e) -> p r u e", u=2),
-                        in0=pairs[:, g].rearrange("p u r e -> p r u e"),
-                        in1=ascale[:, g].unsqueeze(1).to_broadcast([P, P, 2, 2]),
+                        out=grouped_t[:, j].rearrange("p g r (u e) -> p (g r) u e", u=2),
+                        in0=t1[n, j][:].rearrange("p u g r -> p (u g r)").bitcast(BF16).rearrange("p (u q e) -> p q u e", u=2, e=2),
+                        in1=ascale_full[:].rearrange("p g r (u e) -> p (g r) u e", u=2),
                         op=ALU.mult,
                     )
 
-        def quant_attn(n):
+        def quant_attn(n, k):
             codes_t = work.tile([P, 4 * P], U32, name="codes", align_bytes=64)
             planes_t = work.tile([P, 4 * P], U8, name="planes", align_bytes=64)
             codes[n], planes[n] = codes_t, planes_t
-            nc.vector.quantize_mx(out=codes_t[:].bitcast(FP8X4), scales=planes_t[:], in_=grouped[n][:].rearrange("p j g r t -> p (j g r t)"))
+            cols = slice(0, 2 * P * k)
+            nc.vector.quantize_mx(out=codes_t[:, cols].bitcast(FP8X4), scales=planes_t[:, cols], in_=grouped[n][:, 0:k].rearrange("p j g r t -> p (j g r t)"))
 
-        def project(n):
-            for j in range(2):
+        def project(n, k):
+            for j in range(k):
                 acc_t = ps2.tile([P, D], F32, name="acc")
                 acc[n, j] = acc_t
                 for g in range(2):
@@ -159,114 +201,123 @@ def tile_tinyblock_pb_t_w4_kernel(tc, attn_bytes, attn_scale, x, wo_words, wo_sc
                         stop=(g == 1),
                     )
 
-        def add_bo(n):
+        def add_bo(n, k):
             xb_t = work.tile([P, 2, D], F32, name="xb", bufs=3)
             xb[n] = xb_t
-            for j in range(2):
+            for j in range(k):
                 nc.gpsimd.tensor_tensor(out=xb_t[:, j, :], in0=xin[n][:, j, :], in1=bo_b[:], op=ALU.add)
 
-        def residual(n):
+        def residual(n, k):
+            t = GROUPS[n][0]
             xm_t = deep.tile([P, 2, D], F32, name="xm")
             xm[n] = xm_t
-            for j in range(2):
+            for j in reversed(range(k)):
                 nc.vector.tensor_tensor(out=xm_t[:, j, :], in0=acc[n, j][:], in1=xb[n][:, j, :], op=ALU.add)
-            nc.sync.dma_start(out=mid_v[:, 2 * n : 2 * n + 2, :], in_=xm_t[:])
+            nc.sync.dma_start(out=mid_v[:, t : t + k, :], in_=xm_t[:, 0:k, :])
 
-        def squares(n):
+        def squares(n, k):
             ss_t = work.tile([P, 2], F32, name="ss")
             ss[n] = ss_t
-            for j in range(2):
+            for j in reversed(range(k)):
                 junk = work.tile([P, D], BF16, name="junk")
                 nc.scalar.activation(out=junk[:], in_=xm[n][:, j, :], func=ACT.Square, accum_out=ss_t[:, j : j + 1])
 
-        def root(n):
+        def root(n, k):
             ms_t = work.tile([P, 2], F32, name="ms")
             rstd_t = work.tile([P, 2], F32, name="rstd")
             rstd[n] = rstd_t
-            nc.gpsimd.tensor_scalar(out=ms_t[:], in0=ss[n][:], scalar1=1.0 / D, scalar2=EPS, op0=ALU.mult, op1=ALU.add)
-            nc.gpsimd.tensor_tensor(out=rstd_t[:], in0=ms_t[:], in1=half[:], op=ALU.pow)
+            nc.gpsimd.tensor_scalar(out=ms_t[:, 0:k], in0=ss[n][:, 0:k], scalar1=1.0 / D, scalar2=EPS, op0=ALU.mult, op1=ALU.add)
+            nc.gpsimd.tensor_tensor(out=rstd_t[:, 0:k], in0=ms_t[:, 0:k], in1=half[:, 0:k], op=ALU.pow)
 
-        def norm(n):
+        def norm(n, k):
             h_t = work.tile([P, 2, D], BF16, name="h")
             h[n] = h_t
-            for j in range(2):
+            for j in reversed(range(k)):
                 nc.vector.scalar_tensor_tensor(out=h_t[:, j, :], in0=xm[n][:, j, :], scalar=rstd[n][:, j : j + 1], in1=gain[:], op0=ALU.mult, op1=ALU.mult)
 
-        def turn_h(n):
+        def turn_h(n, k):
             bank = ps1.tile([P, 2, 2, P], F32, name="t2")
             t2[n] = bank
-            for j in range(2):
+            for j in reversed(range(k)):
                 words = h[n][:, j, :].bitcast(F32)
                 for u in range(2):
                     nc.tensor.transpose(bank[:, j, u, :], words[:, u:256:2], ident[:])
 
-        def group_h(n):
+        def group_h(n, k):
             h4_t = work.tile([P, 2, P, 4], BF16, name="h4", align_bytes=64)
             h4[n] = h4_t
-            nc.scalar.copy(out=h4_t[:].rearrange("p j r t -> p (j r t)").bitcast(F32).rearrange("p (j r u) -> p j r u", j=2, u=2), in_=t2[n][:].rearrange("p j u r -> p j r u"))
+            nc.scalar.copy(out=h4_t[:].rearrange("p j r t -> p (j r t)").bitcast(F32).rearrange("p (j r u) -> p j r u", j=2, u=2)[:, 0:k], in_=t2[n][:, 0:k].rearrange("p j u r -> p j r u"))
 
-        def quant_h(n):
+        def quant_h(n, k):
             hcodes_t = work.tile([P, 2 * P], U32, name="hcodes", align_bytes=64)
             hplanes_t = work.tile([P, 2 * P], U8, name="hplanes", align_bytes=64)
             hcodes[n], hplanes[n] = hcodes_t, hplanes_t
-            nc.vector.quantize_mx(out=hcodes_t[:].bitcast(FP8X4), scales=hplanes_t[:], in_=h4[n][:].rearrange("p j r t -> p (j r t)"))
+            nc.vector.quantize_mx(out=hcodes_t[:, 0 : P * k].bitcast(FP8X4), scales=hplanes_t[:, 0 : P * k], in_=h4[n][:, 0:k].rearrange("p j r t -> p (j r t)"))
 
-        def expand(n):
+        def expand(n, k):
             bank = ps1.tile([P, 2, 2 * P], F32, name="mx2")
             mx2[n] = bank
             for c in range(2):
                 nc.tensor.matmul_mx(
-                    out=bank[:, c, :],
+                    out=bank[:, c, 0 : P * k],
                     lhsT=w1_t[:, 2 * P * c : 2 * P * (c + 1)].bitcast(FP4X4),
                     lhsT_scale=wplanes[:, 2 * D + P * c : 2 * D + P * (c + 1)],
-                    rhs=hcodes[n][:].bitcast(FP8X4),
-                    rhs_scale=hplanes[n][:],
+                    rhs=hcodes[n][:, 0 : P * k].bitcast(FP8X4),
+                    rhs_scale=hplanes[n][:, 0 : P * k],
                     start=True,
                     stop=True,
                 )
 
-        def gelu(n):
+        def gelu(n, k):
             gt_t = work.tile([P, 2, 2 * P], F32, name="gt")
             gt[n] = gt_t
             for c in range(2):
-                nc.scalar.activation(out=gt_t[:, c, :], in_=mx2[n][:, c, :], func=ACT.Gelu, bias=b1_col[:, c : c + 1])
+                nc.scalar.activation(out=gt_t[:, c, 0 : P * k], in_=mx2[n][:, c, 0 : P * k], func=ACT.Gelu, bias=b1_col[:, c : c + 1])
 
-        def turn_g(n):
+        def turn_g(n, k):
             bank = ps1.tile([P, 2, 2, P], F32, name="t3")
             t3[n] = bank
-            for j in range(2):
+            for j in range(k):
                 for c in range(2):
                     nc.tensor.transpose(bank[:, j, c, :], gt[n][:, c, P * j : P * (j + 1)], ident[:])
 
-        def store_g(n):
+        def store_g(n, k):
+            t = GROUPS[n][0]
             g_t = work.tile([P, 2, F], F32, name="g", bufs=3)
-            nc.scalar.copy(out=g_t[:].rearrange("p j f -> p (j f)"), in_=t3[n][:].rearrange("p j c r -> p (j c r)"))
-            nc.sync.dma_start(out=g_v[:, 2 * n : 2 * n + 2, :], in_=g_t[:])
+            nc.scalar.copy(out=g_t[:, 0:k, :], in_=t3[n][:, 0:k].rearrange("p j c r -> p j (c r)"))
+            nc.sync.dma_start(out=g_v[:, t : t + k, :], in_=g_t[:, 0:k, :])
 
-        def run(stage, n):
-            if 0 <= n < PAIRS:
-                stage(n)
-
-        cast(0)
-        turn_attn(0)
-        cast(1)
-        vectors()
-        add_bo(0)
-        for n in range(PAIRS + 4):
-            run(scale_attn, n)
-            run(gelu, n - 4)
-            run(cast, n + 2)
-            run(turn_h, n - 3)
-            run(turn_g, n - 4)
-            run(turn_attn, n + 1)
-            run(group_h, n - 3)
-            run(store_g, n - 4)
-            run(residual, n - 1)
-            run(squares, n - 1)
-            run(add_bo, n + 1)
-            run(root, n - 1)
-            run(quant_h, n - 3)
-            run(quant_attn, n)
-            run(expand, n - 3)
-            run(project, n)
-            run(norm, n - 2)
+        stages = {
+            "gpsimd_scale": gpsimd_scale,
+            "scale_attn": scale_attn,
+            "residual": residual,
+            "cast": cast,
+            "gelu": gelu,
+            "turn_h": turn_h,
+            "turn_g": turn_g,
+            "turn_attn": turn_attn,
+            "group_h": group_h,
+            "squares": squares,
+            "add_bo": add_bo,
+            "store_g": store_g,
+            "root": root,
+            "quant_h": quant_h,
+            "quant_attn": quant_attn,
+            "expand": expand,
+            "project": project,
+            "norm": norm,
+        }
+        lead = [max([0] + [lag for s, lag in STEPS if s == name]) for name in ("cast", "gpsimd_scale", "turn_attn")]
+        done = set()
+        for n in range(max(lead)):
+            for name, ahead in zip(("cast", "gpsimd_scale", "turn_attn"), lead):
+                if n < ahead:
+                    stages[name](n, len(GROUPS[n]))
+                    done.add((name, n))
+            if n == 0:
+                vectors()
+        for step in range(len(GROUPS) + 4):
+            for name, lag in STEPS:
+                n = step + lag
+                if 0 <= n < len(GROUPS) and (name, n) not in done:
+                    stages[name](n, len(GROUPS[n]))

@@ -18,26 +18,24 @@ TOKENS, E, D, F = 4096, 1024, 512, 256
 EPS = 1e-6
 P = 128
 TILES = TOKENS // P
-GROUPS = [[0], [1]] + [[t, t + 1] for t in range(2, TILES - 2, 2)] + [[TILES - 2], [TILES - 1]]
-ON_GPSIMD = (7, 12, 17, 22, 27)
+GROUPS = [[0]] + [[t, t + 1] for t in range(1, TILES - 1, 2)] + [[TILES - 1]]
 STEPS = [
-    ("gpsimd_scale", 1),
-    ("scale_attn", 0),
-    ("residual", -1),
-    ("cast", 2),
     ("gelu", -4),
     ("turn_h", -3),
+    ("scale_attn", 0),
     ("turn_g", -4),
+    ("residual", -1),
+    ("quant_attn", 0),
     ("turn_attn", 1),
     ("group_h", -3),
-    ("squares", -1),
-    ("add_bo", 0),
-    ("store_g", -4),
-    ("root", -1),
+    ("root", -2),
     ("quant_h", -3),
-    ("quant_attn", 0),
-    ("expand", -3),
+    ("squares", -1),
+    ("store_g", -4),
+    ("cast", 2),
     ("project", 0),
+    ("expand", -3),
+    ("add_bo", 0),
     ("norm", -2),
 ]
 FLOPS = 2 * TOKENS * E * D + 2 * TOKENS * D * F
@@ -93,9 +91,9 @@ def tile_tinyblock_pb_t_w4_kernel(tc, attn_bytes, attn_scale, x, wo_words, wo_sc
             nc.sync.dma_start(out=xin[n][:, 0:k, :], in_=x_v[:, t : t + k, :])
 
         load_bytes(0)
-        load_bytes(1)
         ascale = const.tile([P, 2, 4], F32, name="ascale")
         nc.sync.dma_start(out=ascale[:], in_=attn_scale.rearrange("a b (g p t) -> p (a b g) t", p=P, t=4))
+        load_bytes(1)
         wo_t = const.tile([P, 4 * D], U8, name="wo_t", align_bytes=64)
         nc.sync.dma_start(out=wo_t[:].bitcast(I32).rearrange("p (g w) -> p g w", g=2), in_=wo_words.bitcast(I32).rearrange("g p w -> p g w"))
         for q in range(4):
@@ -108,14 +106,8 @@ def tile_tinyblock_pb_t_w4_kernel(tc, attn_bytes, attn_scale, x, wo_words, wo_sc
         w1_t = const.tile([P, 2 * F], U8, name="w1_t", align_bytes=64)
         nc.sync.dma_start(out=w1_t[:].bitcast(I32), in_=w1_words[0].bitcast(I32))
         load_x(0)
-        load_bytes(2)
         load_x(1)
-        load_bytes(3)
-        load_x(2)
-        ascale_row = const.tile([P, E], F32, name="ascale_row")
-        nc.sync.dma_start(out=ascale_row[:], in_=attn_scale.rearrange("a b k -> (a b k)").partition_broadcast(P))
-        load_x(3)
-        for n in range(4, len(GROUPS)):
+        for n in range(2, len(GROUPS)):
             load_bytes(n)
             load_x(n)
 
@@ -137,26 +129,17 @@ def tile_tinyblock_pb_t_w4_kernel(tc, attn_bytes, attn_scale, x, wo_words, wo_sc
 
         a16, t1, codes, planes, acc, xb, xm, ss, rstd = {}, {}, {}, {}, {}, {}, {}, {}, {}
         grouped, h, t2, h4, hcodes, hplanes, mx2, gt, t3 = {}, {}, {}, {}, {}, {}, {}, {}, {}
-        scaled = {}
 
         def cast(n, k):
             a16_t = work.tile([P, 2, E], BF16, name="a16", bufs=3)
             a16[n] = a16_t
             nc.scalar.copy(out=a16_t[:, 0:k, :], in_=abytes[n][:, 0:k, :].bitcast(FP8))
 
-        def gpsimd_scale(n, k):
-            for j, t in enumerate(GROUPS[n]):
-                if t in ON_GPSIMD:
-                    scaled_t = work.tile([P, E], BF16, name="scaled")
-                    scaled[t] = scaled_t
-                    nc.gpsimd.tensor_tensor(out=scaled_t[:], in0=a16[n][:, j, :], in1=ascale_row[:], op=ALU.mult)
-
         def turn_attn(n, k):
-            for j, t in enumerate(GROUPS[n]):
+            for j in range(k):
                 bank = ps2.tile([P, 2, 2, P], F32, name="t1")
                 t1[n, j] = bank
-                source = scaled[t][:] if t in ON_GPSIMD else a16[n][:, j, :]
-                words = source.bitcast(F32)
+                words = a16[n][:, j, :].bitcast(F32)
                 for g in range(2):
                     for u in range(2):
                         nc.tensor.transpose(bank[:, u, g, :], words[:, 256 * g + u : 256 * (g + 1) : 2], ident[:])
@@ -165,18 +148,12 @@ def tile_tinyblock_pb_t_w4_kernel(tc, attn_bytes, attn_scale, x, wo_words, wo_sc
             grouped_t = work.tile([P, 2, 2, P, 4], BF16, name="grouped", align_bytes=64)
             grouped[n] = grouped_t
             for j in reversed(range(k)):
-                if GROUPS[n][j] in ON_GPSIMD:
-                    nc.scalar.copy(
-                        out=grouped_t[:, j].rearrange("p g r t -> p (g r t)").bitcast(F32).rearrange("p (q u) -> p q u", u=2),
-                        in_=t1[n, j][:].rearrange("p u g r -> p (g r) u"),
-                    )
-                else:
-                    nc.vector.tensor_tensor(
-                        out=grouped_t[:, j].rearrange("p g r (u e) -> p (g r) u e", u=2),
-                        in0=t1[n, j][:].rearrange("p u g r -> p (u g r)").bitcast(BF16).rearrange("p (u q e) -> p q u e", u=2, e=2),
-                        in1=ascale_full[:].rearrange("p g r (u e) -> p (g r) u e", u=2),
-                        op=ALU.mult,
-                    )
+                nc.vector.tensor_tensor(
+                    out=grouped_t[:, j].rearrange("p g r (u e) -> p (g r) u e", u=2),
+                    in0=t1[n, j][:].rearrange("p u g r -> p (u g r)").bitcast(BF16).rearrange("p (u q e) -> p q u e", u=2, e=2),
+                    in1=ascale_full[:].rearrange("p g r (u e) -> p (g r) u e", u=2),
+                    op=ALU.mult,
+                )
 
         def quant_attn(n, k):
             codes_t = work.tile([P, 4 * P], U32, name="codes", align_bytes=64)
@@ -216,15 +193,15 @@ def tile_tinyblock_pb_t_w4_kernel(tc, attn_bytes, attn_scale, x, wo_words, wo_sc
             nc.sync.dma_start(out=mid_v[:, t : t + k, :], in_=xm_t[:, 0:k, :])
 
         def squares(n, k):
-            ss_t = work.tile([P, 2], F32, name="ss")
+            ss_t = work.tile([P, 2], F32, name="ss", bufs=4)
             ss[n] = ss_t
             for j in reversed(range(k)):
                 junk = work.tile([P, D], BF16, name="junk")
                 nc.scalar.activation(out=junk[:], in_=xm[n][:, j, :], func=ACT.Square, accum_out=ss_t[:, j : j + 1])
 
         def root(n, k):
-            ms_t = work.tile([P, 2], F32, name="ms")
-            rstd_t = work.tile([P, 2], F32, name="rstd")
+            ms_t = work.tile([P, 2], F32, name="ms", bufs=4)
+            rstd_t = work.tile([P, 2], F32, name="rstd", bufs=4)
             rstd[n] = rstd_t
             nc.gpsimd.tensor_scalar(out=ms_t[:, 0:k], in0=ss[n][:, 0:k], scalar1=1.0 / D, scalar2=EPS, op0=ALU.mult, op1=ALU.add)
             nc.gpsimd.tensor_tensor(out=rstd_t[:, 0:k], in0=ms_t[:, 0:k], in1=half[:, 0:k], op=ALU.pow)
@@ -288,7 +265,6 @@ def tile_tinyblock_pb_t_w4_kernel(tc, attn_bytes, attn_scale, x, wo_words, wo_sc
             nc.sync.dma_start(out=g_v[:, t : t + k, :], in_=g_t[:, 0:k, :])
 
         stages = {
-            "gpsimd_scale": gpsimd_scale,
             "scale_attn": scale_attn,
             "residual": residual,
             "cast": cast,
@@ -307,17 +283,13 @@ def tile_tinyblock_pb_t_w4_kernel(tc, attn_bytes, attn_scale, x, wo_words, wo_sc
             "project": project,
             "norm": norm,
         }
-        lead = [max([0] + [lag for s, lag in STEPS if s == name]) for name in ("cast", "gpsimd_scale", "turn_attn")]
-        done = set()
-        for n in range(max(lead)):
-            for name, ahead in zip(("cast", "gpsimd_scale", "turn_attn"), lead):
-                if n < ahead:
-                    stages[name](n, len(GROUPS[n]))
-                    done.add((name, n))
-            if n == 0:
-                vectors()
+        cast(0, len(GROUPS[0]))
+        turn_attn(0, len(GROUPS[0]))
+        cast(1, len(GROUPS[1]))
+        vectors()
+        early = {("cast", 0), ("cast", 1), ("turn_attn", 0)}
         for step in range(len(GROUPS) + 4):
             for name, lag in STEPS:
                 n = step + lag
-                if 0 <= n < len(GROUPS) and (name, n) not in done:
+                if 0 <= n < len(GROUPS) and (name, n) not in early:
                     stages[name](n, len(GROUPS[n]))

@@ -40,6 +40,40 @@ STEPS = [
 ]
 FLOPS = 2 * TOKENS * E * D + 2 * TOKENS * D * F
 
+DRAIN = [
+    ("turn_h", 14),
+    ("root", 15),
+    ("gelu", 13),
+    ("residual", 16),
+    ("group_h", 14),
+    ("norm", 15),
+    ("turn_g", 13),
+    ("turn_h", 15),
+    ("squares", 16),
+    ("quant_h", 14),
+    ("store_g", 13),
+    ("root", 16),
+    ("group_h", 15),
+    ("expand", 14),
+    ("quant_h", 15),
+    ("gelu", 14),
+    ("expand", 15),
+    ("norm", 16),
+    ("gelu", 15),
+    ("turn_g", 14),
+    ("turn_h", 16),
+    ("store_g", 14),
+    ("group_h", 16),
+    ("quant_h", 16),
+    ("turn_g", 15),
+    ("store_g", 15),
+    ("expand", 16),
+    ("gelu", 16),
+    ("turn_g", 16),
+    ("store_g", 16),
+]
+ON_VECTOR = {("group_h", 15), ("store_g", 14), ("store_g", 15)}
+
 
 def tile_tinyblock_pb_t_w4_kernel(tc, attn_bytes, attn_scale, x, wo_words, wo_scales, bo, mlp_norm_w, w1_words, w1_scales, b1, out_0, out_1):
     nc = tc.nc
@@ -65,10 +99,12 @@ def tile_tinyblock_pb_t_w4_kernel(tc, attn_bytes, attn_scale, x, wo_words, wo_sc
         make_identity(nc, ident[:])
         wplanes = const.tile([P, 2 * D + F], U8, name="wplanes", align_bytes=64)
         nc.vector.memset(wplanes[:].bitcast(I32), 0)
-        rows = const.tile([P, 2 * D + F], BF16, name="rows")
-        nc.vector.memset(rows[:], 0.0)
         ones = const.tile([P, P], BF16, name="ones")
         nc.vector.memset(ones[:], 1.0)
+        filler = const.tile([P, D], BF16, name="filler")
+        nc.vector.memset(filler[:], 0.0)
+        rows = const.tile([P, 2 * D + F], BF16, name="rows")
+        nc.vector.memset(rows[:], 0.0)
         half = const.tile([P, 2], F32, name="half")
         nc.vector.memset(half[:], -0.5)
 
@@ -90,50 +126,83 @@ def tile_tinyblock_pb_t_w4_kernel(tc, attn_bytes, attn_scale, x, wo_words, wo_sc
             t = GROUPS[n][0]
             nc.sync.dma_start(out=xin[n][:, 0:k, :], in_=x_v[:, t : t + k, :])
 
+        ascale = const.tile([P, 2, 2, 2], F32, name="ascale")
+        nc.sync.dma_start(out=ascale[:].rearrange("p g u e -> p g (u e)"), in_=attn_scale.rearrange("a b (g p t) -> p (a b g) t", p=P, t=4))
         load_bytes(0)
-        ascale = const.tile([P, 2, 4], F32, name="ascale")
-        nc.sync.dma_start(out=ascale[:], in_=attn_scale.rearrange("a b (g p t) -> p (a b g) t", p=P, t=4))
-        load_bytes(1)
         wo_t = const.tile([P, 4 * D], U8, name="wo_t", align_bytes=64)
-        nc.sync.dma_start(out=wo_t[:].bitcast(I32).rearrange("p (g w) -> p g w", g=2), in_=wo_words.bitcast(I32).rearrange("g p w -> p g w"))
         for q in range(4):
             nc.sync.dma_start(out=wplanes[32 * q : 32 * q + 4, 0 : 2 * D].bitcast(I32).rearrange("q (g n) -> q g n", g=2), in_=wo_scales[:, 4 * q : 4 * q + 4, :].bitcast(I32).rearrange("g q n -> q g n"))
-        for q in range(4):
-            nc.sync.dma_start(out=wplanes[32 * q : 32 * q + 4, 2 * D : 2 * D + F].bitcast(I32), in_=w1_scales[0, 4 * q : 4 * q + 4, :].bitcast(I32))
+        load_bytes(1)
+        nc.sync.dma_start(out=wo_t[:].bitcast(I32).rearrange("p (g w) -> p g w", g=2), in_=wo_words.bitcast(I32).rearrange("g p w -> p g w"))
         nc.sync.dma_start(out=rows[0:1, 0:D], in_=bo.unsqueeze(0))
+        load_x(0)
+        load_bytes(2)
+        load_x(1)
         nc.sync.dma_start(out=rows[0:1, D : 2 * D], in_=mlp_norm_w.unsqueeze(0))
         nc.sync.dma_start(out=rows[0:1, 2 * D : 2 * D + F], in_=b1.unsqueeze(0))
+        load_bytes(3)
+        load_x(2)
         w1_t = const.tile([P, 2 * F], U8, name="w1_t", align_bytes=64)
         nc.sync.dma_start(out=w1_t[:].bitcast(I32), in_=w1_words[0].bitcast(I32))
-        load_x(0)
-        load_x(1)
-        for n in range(2, len(GROUPS)):
+        for q in range(4):
+            nc.sync.dma_start(out=wplanes[32 * q : 32 * q + 4, 2 * D : 2 * D + F].bitcast(I32), in_=w1_scales[0, 4 * q : 4 * q + 4, :].bitcast(I32))
+        load_x(3)
+        for n in range(4, len(GROUPS)):
             load_bytes(n)
             load_x(n)
 
         ascale_full = const.tile([P, 2, P, 4], F32, name="ascale_full")
-        nc.vector.tensor_copy(out=ascale_full[:], in_=ascale[:].unsqueeze(2).to_broadcast([P, 2, P, 4]))
+        nc.gpsimd.tensor_scalar(out=ascale_full[:], in0=ascale[:].rearrange("p g u e -> p g (u e)").unsqueeze(2).to_broadcast([P, 2, P, 4]), scalar1=1.0, scalar2=0.0, op0=ALU.mult, op1=ALU.add)
         gain = ps1.tile([P, D], F32, name="gain")
         bo_b = const.tile([P, D], BF16, name="bo_b")
         b1_col = const.tile([P, 2], F32, name="b1_col")
 
-        def vectors():
-            nc.tensor.matmul(gain[:], lhsT=ones[:], rhs=rows[:, D : 2 * D], start=True, stop=True)
-            spread = ps2.tile([P, D], F32, name="acc")
-            nc.tensor.matmul(spread[:], lhsT=ones[:], rhs=rows[:, 0:D], start=True, stop=True)
-            nc.scalar.copy(out=bo_b[:], in_=spread[:])
-            col = ps1.tile([P, 2, F], F32, name="mx2")
-            for c in range(2):
-                nc.tensor.matmul(col[:, c, 0:8], lhsT=rows[:, 2 * D + P * c : 2 * D + P * (c + 1)], rhs=ones[:, 0:8], start=True, stop=True)
-            nc.scalar.copy(out=b1_col[:], in_=col[:, :, 0])
+        def warm_up():
+            bank = ps1.tile([P, D], F32, name="t2")
+            for i in range(4):
+                nc.tensor.matmul(bank[:], lhsT=ones[:], rhs=filler[:], start=True, stop=True)
 
-        a16, t1, codes, planes, acc, xb, xm, ss, rstd = {}, {}, {}, {}, {}, {}, {}, {}, {}
+        def spread_bo():
+            bank = ps2.tile([P, D], F32, name="acc")
+            nc.tensor.matmul(bank[:], lhsT=ones[:], rhs=rows[:, 0:D], start=True, stop=True)
+            nc.scalar.copy(out=bo_b[:], in_=bank[:])
+
+        def spread_gain_b1():
+            nc.tensor.matmul(gain[:], lhsT=ones[:], rhs=rows[:, D : 2 * D], start=True, stop=True)
+            bank = ps1.tile([P, 2, F], F32, name="mx2")
+            for c in range(2):
+                nc.tensor.matmul(bank[:, c, 0:8], lhsT=rows[:, 2 * D + P * c : 2 * D + P * (c + 1)], rhs=ones[:, 0:8], start=True, stop=True)
+            nc.scalar.copy(out=b1_col[:], in_=bank[:, :, 0])
+
+        a16, t1, codes, planes, acc, xb, xm, ms, rstd = {}, {}, {}, {}, {}, {}, {}, {}, {}
         grouped, h, t2, h4, hcodes, hplanes, mx2, gt, t3 = {}, {}, {}, {}, {}, {}, {}, {}, {}
 
         def cast(n, k):
             a16_t = work.tile([P, 2, E], BF16, name="a16", bufs=3)
             a16[n] = a16_t
             nc.scalar.copy(out=a16_t[:, 0:k, :], in_=abytes[n][:, 0:k, :].bitcast(FP8))
+
+        def first_tile():
+            a16_t = work.tile([P, 2, E], BF16, name="a16", bufs=3)
+            for g in range(2):
+                k_cols = slice(512 * g, 512 * (g + 1))
+                nc.scalar.copy(out=a16_t[:, 0, k_cols], in_=abytes[0][:, 0, k_cols].bitcast(FP8))
+            banks = []
+            for g in range(2):
+                bank = ps2.tile([P, 2, P], F32, name="t1")
+                banks.append(bank)
+                words = a16_t[:, 0, :].bitcast(F32)
+                for u in range(2):
+                    nc.tensor.transpose(bank[:, u, :], words[:, 256 * g + u : 256 * (g + 1) : 2], ident[:])
+            grouped_t = work.tile([P, 2, 2, P, 4], BF16, name="grouped", align_bytes=64)
+            grouped[0] = grouped_t
+            for g in range(2):
+                nc.vector.tensor_tensor(
+                    out=grouped_t[:, 0, g].rearrange("p r (u e) -> p r u e", u=2),
+                    in0=banks[g][:].rearrange("p u r -> p (u r)").bitcast(BF16).rearrange("p (u r e) -> p r u e", u=2, e=2),
+                    in1=ascale[:, g].unsqueeze(1).to_broadcast([P, P, 2, 2]),
+                    op=ALU.mult,
+                )
 
         def turn_attn(n, k):
             for j in range(k):
@@ -194,17 +263,17 @@ def tile_tinyblock_pb_t_w4_kernel(tc, attn_bytes, attn_scale, x, wo_words, wo_sc
 
         def squares(n, k):
             ss_t = work.tile([P, 2], F32, name="ss", bufs=4)
-            ss[n] = ss_t
             for j in reversed(range(k)):
                 junk = work.tile([P, D], BF16, name="junk")
                 nc.scalar.activation(out=junk[:], in_=xm[n][:, j, :], func=ACT.Square, accum_out=ss_t[:, j : j + 1])
+            ms_t = work.tile([P, 2], F32, name="ms", bufs=4)
+            ms[n] = ms_t
+            nc.scalar.activation(out=ms_t[:, 0:k], in_=ss_t[:, 0:k], func=ACT.Copy, scale=1.0 / D, bias=EPS)
 
         def root(n, k):
-            ms_t = work.tile([P, 2], F32, name="ms", bufs=4)
             rstd_t = work.tile([P, 2], F32, name="rstd", bufs=4)
             rstd[n] = rstd_t
-            nc.gpsimd.tensor_scalar(out=ms_t[:, 0:k], in0=ss[n][:, 0:k], scalar1=1.0 / D, scalar2=EPS, op0=ALU.mult, op1=ALU.add)
-            nc.gpsimd.tensor_tensor(out=rstd_t[:, 0:k], in0=ms_t[:, 0:k], in1=half[:, 0:k], op=ALU.pow)
+            nc.gpsimd.tensor_tensor(out=rstd_t[:, 0:k], in0=ms[n][:, 0:k], in1=half[:, 0:k], op=ALU.pow)
 
         def norm(n, k):
             h_t = work.tile([P, 2, D], BF16, name="h")
@@ -223,7 +292,8 @@ def tile_tinyblock_pb_t_w4_kernel(tc, attn_bytes, attn_scale, x, wo_words, wo_sc
         def group_h(n, k):
             h4_t = work.tile([P, 2, P, 4], BF16, name="h4", align_bytes=64)
             h4[n] = h4_t
-            nc.scalar.copy(out=h4_t[:].rearrange("p j r t -> p (j r t)").bitcast(F32).rearrange("p (j r u) -> p j r u", j=2, u=2)[:, 0:k], in_=t2[n][:, 0:k].rearrange("p j u r -> p j r u"))
+            copy = nc.vector.tensor_copy if ("group_h", n) in ON_VECTOR else nc.scalar.copy
+            copy(out=h4_t[:].rearrange("p j r t -> p (j r t)").bitcast(F32).rearrange("p (j r u) -> p j r u", j=2, u=2)[:, 0:k], in_=t2[n][:, 0:k].rearrange("p j u r -> p j r u"))
 
         def quant_h(n, k):
             hcodes_t = work.tile([P, 2 * P], U32, name="hcodes", align_bytes=64)
@@ -261,7 +331,8 @@ def tile_tinyblock_pb_t_w4_kernel(tc, attn_bytes, attn_scale, x, wo_words, wo_sc
         def store_g(n, k):
             t = GROUPS[n][0]
             g_t = work.tile([P, 2, F], F32, name="g", bufs=3)
-            nc.scalar.copy(out=g_t[:, 0:k, :], in_=t3[n][:, 0:k].rearrange("p j c r -> p j (c r)"))
+            copy = nc.vector.tensor_copy if ("store_g", n) in ON_VECTOR else nc.scalar.copy
+            copy(out=g_t[:, 0:k, :], in_=t3[n][:, 0:k].rearrange("p j c r -> p j (c r)"))
             nc.sync.dma_start(out=g_v[:, t : t + k, :], in_=g_t[:, 0:k, :])
 
         stages = {
@@ -283,13 +354,18 @@ def tile_tinyblock_pb_t_w4_kernel(tc, attn_bytes, attn_scale, x, wo_words, wo_sc
             "project": project,
             "norm": norm,
         }
-        cast(0, len(GROUPS[0]))
-        turn_attn(0, len(GROUPS[0]))
+        warm_up()
+        first_tile()
         cast(1, len(GROUPS[1]))
-        vectors()
-        early = {("cast", 0), ("cast", 1), ("turn_attn", 0)}
-        for step in range(len(GROUPS) + 4):
+        early = {("cast", 0), ("cast", 1), ("turn_attn", 0), ("scale_attn", 0)}
+        for step in range(len(GROUPS)):
             for name, lag in STEPS:
                 n = step + lag
+                if (name, n) == ("project", 0):
+                    spread_bo()
                 if 0 <= n < len(GROUPS) and (name, n) not in early:
                     stages[name](n, len(GROUPS[n]))
+                if (name, n) == ("project", 1):
+                    spread_gain_b1()
+        for name, n in DRAIN:
+            stages[name](n, len(GROUPS[n]))

from contextlib import ExitStack

import concourse.mybir as mybir
from concourse.masks import make_identity

F32 = mybir.dt.float32
BF16 = mybir.dt.bfloat16
I32 = mybir.dt.int32
U32 = mybir.dt.uint32
U8 = mybir.dt.uint8
FP8 = mybir.dt.float8_e4m3fn
FP8X4 = mybir.dt.float8_e4m3fn_x4
FP4X4 = mybir.dt.float4_e2m1fn_x4
ACT = mybir.ActivationFunctionType
ALU = mybir.AluOpType

TOKENS, E, D, F = 4096, 1024, 512, 256
EPS = 1e-6
P = 128
TILES = TOKENS // P
GROUPS = [[0]] + [[t, t + 1] for t in range(1, TILES - 1, 2)] + [[TILES - 1]]
STEPS = [
    ("gelu", -4),
    ("turn_h", -3),
    ("scale_attn", 0),
    ("turn_g", -4),
    ("residual", -1),
    ("quant_attn", 0),
    ("turn_attn", 1),
    ("group_h", -3),
    ("root", -2),
    ("quant_h", -3),
    ("squares", -1),
    ("store_g", -4),
    ("cast", 2),
    ("project", 0),
    ("expand", -3),
    ("add_bo", 0),
    ("norm", -2),
]
FLOPS = 2 * TOKENS * E * D + 2 * TOKENS * D * F

DRAIN = [
    ("turn_h", 14),
    ("root", 15),
    ("gelu", 13),
    ("residual", 16),
    ("group_h", 14),
    ("norm", 15),
    ("turn_g", 13),
    ("turn_h", 15),
    ("squares", 16),
    ("quant_h", 14),
    ("store_g", 13),
    ("root", 16),
    ("group_h", 15),
    ("expand", 14),
    ("quant_h", 15),
    ("gelu", 14),
    ("expand", 15),
    ("norm", 16),
    ("gelu", 15),
    ("turn_g", 14),
    ("turn_h", 16),
    ("store_g", 14),
    ("group_h", 16),
    ("quant_h", 16),
    ("turn_g", 15),
    ("store_g", 15),
    ("expand", 16),
    ("gelu", 16),
    ("turn_g", 16),
    ("store_g", 16),
]
ON_VECTOR = {("group_h", 15), ("store_g", 14), ("store_g", 15)}


def tile_tinyblock_pb_t_w4_kernel(tc, attn_bytes, attn_scale, x, wo_words, wo_scales, bo, mlp_norm_w, w1_words, w1_scales, b1, out_0, out_1):
    nc = tc.nc
    bytes_v = attn_bytes.flatten_outer_dims().rearrange("(p j) k -> p j k", j=TILES)
    x_v = x.flatten_outer_dims().rearrange("(p j) d -> p j d", j=TILES)
    mid_v = out_0.flatten_outer_dims().rearrange("(p j) d -> p j d", j=TILES)
    g_v = out_1.flatten_outer_dims().rearrange("(p j) f -> p j f", j=TILES)

    with ExitStack() as ctx:
        const = ctx.enter_context(tc.tile_pool(name="const", bufs=1))
        keep = ctx.enter_context(tc.tile_pool(name="keep", bufs=len(GROUPS)))
        work = ctx.enter_context(tc.tile_pool(name="work", bufs=2))
        deep = ctx.enter_context(tc.tile_pool(name="deep", bufs=5))
        ps2 = ctx.enter_context(tc.psum_pool(name="ps2", bufs=2))
        ps1 = ctx.enter_context(tc.psum_pool(name="ps1", bufs=1))
        ctx.enter_context(tc.manual_schedule())

        warm = const.tile([P, 1], F32, name="warm")
        nc.vector.memset(warm[:], 0.0)
        warm_out = const.tile([P, 1], F32, name="warm_out")
        nc.scalar.activation(out=warm_out[:], in_=warm[:], func=ACT.Gelu)
        ident = const.tile([P, P], F32, name="ident")
        make_identity(nc, ident[:])
        wplanes = const.tile([P, 2 * D + F], U8, name="wplanes", align_bytes=64)
        nc.vector.memset(wplanes[:].bitcast(I32), 0)
        ones = const.tile([P, P], BF16, name="ones")
        nc.vector.memset(ones[:], 1.0)
        filler = const.tile([P, D], BF16, name="filler")
        nc.vector.memset(filler[:], 0.0)
        rows = const.tile([P, 2 * D + F], BF16, name="rows")
        nc.vector.memset(rows[:], 0.0)
        half = const.tile([P, 2], F32, name="half")
        nc.vector.memset(half[:], -0.5)

        abytes = []
        xin = []
        for tiles in GROUPS:
            abytes_t = keep.tile([P, 2, E], U8, name="abytes")
            xin_t = keep.tile([P, 2, D], BF16, name="xin")
            abytes.append(abytes_t)
            xin.append(xin_t)

        def load_bytes(n):
            k = len(GROUPS[n])
            t = GROUPS[n][0]
            nc.sync.dma_start(out=abytes[n][:, 0:k, :], in_=bytes_v[:, t : t + k, :])

        def load_x(n):
            k = len(GROUPS[n])
            t = GROUPS[n][0]
            nc.sync.dma_start(out=xin[n][:, 0:k, :], in_=x_v[:, t : t + k, :])

        ascale = const.tile([P, 2, 2, 2], F32, name="ascale")
        nc.sync.dma_start(out=ascale[:].rearrange("p g u e -> p g (u e)"), in_=attn_scale.rearrange("a b (g p t) -> p (a b g) t", p=P, t=4))
        load_bytes(0)
        wo_t = const.tile([P, 4 * D], U8, name="wo_t", align_bytes=64)
        for q in range(4):
            nc.sync.dma_start(out=wplanes[32 * q : 32 * q + 4, 0 : 2 * D].bitcast(I32).rearrange("q (g n) -> q g n", g=2), in_=wo_scales[:, 4 * q : 4 * q + 4, :].bitcast(I32).rearrange("g q n -> q g n"))
        load_bytes(1)
        nc.sync.dma_start(out=wo_t[:].bitcast(I32).rearrange("p (g w) -> p g w", g=2), in_=wo_words.bitcast(I32).rearrange("g p w -> p g w"))
        nc.sync.dma_start(out=rows[0:1, 0:D], in_=bo.unsqueeze(0))
        load_x(0)
        load_bytes(2)
        load_x(1)
        nc.sync.dma_start(out=rows[0:1, D : 2 * D], in_=mlp_norm_w.unsqueeze(0))
        nc.sync.dma_start(out=rows[0:1, 2 * D : 2 * D + F], in_=b1.unsqueeze(0))
        load_bytes(3)
        load_x(2)
        w1_t = const.tile([P, 2 * F], U8, name="w1_t", align_bytes=64)
        nc.sync.dma_start(out=w1_t[:].bitcast(I32), in_=w1_words[0].bitcast(I32))
        for q in range(4):
            nc.sync.dma_start(out=wplanes[32 * q : 32 * q + 4, 2 * D : 2 * D + F].bitcast(I32), in_=w1_scales[0, 4 * q : 4 * q + 4, :].bitcast(I32))
        load_x(3)
        for n in range(4, len(GROUPS)):
            load_bytes(n)
            load_x(n)

        ascale_full = const.tile([P, 2, P, 4], F32, name="ascale_full")
        nc.gpsimd.tensor_scalar(out=ascale_full[:], in0=ascale[:].rearrange("p g u e -> p g (u e)").unsqueeze(2).to_broadcast([P, 2, P, 4]), scalar1=1.0, scalar2=0.0, op0=ALU.mult, op1=ALU.add)
        gain = ps1.tile([P, D], F32, name="gain")
        bo_b = const.tile([P, D], BF16, name="bo_b")
        b1_col = const.tile([P, 2], F32, name="b1_col")

        def warm_up():
            bank = ps1.tile([P, D], F32, name="t2")
            for i in range(4):
                nc.tensor.matmul(bank[:], lhsT=ones[:], rhs=filler[:], start=True, stop=True)

        def spread_bo():
            bank = ps2.tile([P, D], F32, name="acc")
            nc.tensor.matmul(bank[:], lhsT=ones[:], rhs=rows[:, 0:D], start=True, stop=True)
            nc.scalar.copy(out=bo_b[:], in_=bank[:])

        def spread_gain_b1():
            nc.tensor.matmul(gain[:], lhsT=ones[:], rhs=rows[:, D : 2 * D], start=True, stop=True)
            bank = ps1.tile([P, 2, F], F32, name="mx2")
            for c in range(2):
                nc.tensor.matmul(bank[:, c, 0:8], lhsT=rows[:, 2 * D + P * c : 2 * D + P * (c + 1)], rhs=ones[:, 0:8], start=True, stop=True)
            nc.scalar.copy(out=b1_col[:], in_=bank[:, :, 0])

        a16, t1, codes, planes, acc, xb, xm, ms, rstd = {}, {}, {}, {}, {}, {}, {}, {}, {}
        grouped, h, t2, h4, hcodes, hplanes, mx2, gt, t3 = {}, {}, {}, {}, {}, {}, {}, {}, {}

        def cast(n, k):
            a16_t = work.tile([P, 2, E], BF16, name="a16", bufs=3)
            a16[n] = a16_t
            nc.scalar.copy(out=a16_t[:, 0:k, :], in_=abytes[n][:, 0:k, :].bitcast(FP8))

        def first_tile():
            a16_t = work.tile([P, 2, E], BF16, name="a16", bufs=3)
            for g in range(2):
                k_cols = slice(512 * g, 512 * (g + 1))
                nc.scalar.copy(out=a16_t[:, 0, k_cols], in_=abytes[0][:, 0, k_cols].bitcast(FP8))
            banks = []
            for g in range(2):
                bank = ps2.tile([P, 2, P], F32, name="t1")
                banks.append(bank)
                words = a16_t[:, 0, :].bitcast(F32)
                for u in range(2):
                    nc.tensor.transpose(bank[:, u, :], words[:, 256 * g + u : 256 * (g + 1) : 2], ident[:])
            grouped_t = work.tile([P, 2, 2, P, 4], BF16, name="grouped", align_bytes=64)
            grouped[0] = grouped_t
            for g in range(2):
                nc.vector.tensor_tensor(
                    out=grouped_t[:, 0, g].rearrange("p r (u e) -> p r u e", u=2),
                    in0=banks[g][:].rearrange("p u r -> p (u r)").bitcast(BF16).rearrange("p (u r e) -> p r u e", u=2, e=2),
                    in1=ascale[:, g].unsqueeze(1).to_broadcast([P, P, 2, 2]),
                    op=ALU.mult,
                )

        def turn_attn(n, k):
            for j in range(k):
                bank = ps2.tile([P, 2, 2, P], F32, name="t1")
                t1[n, j] = bank
                words = a16[n][:, j, :].bitcast(F32)
                for g in range(2):
                    for u in range(2):
                        nc.tensor.transpose(bank[:, u, g, :], words[:, 256 * g + u : 256 * (g + 1) : 2], ident[:])

        def scale_attn(n, k):
            grouped_t = work.tile([P, 2, 2, P, 4], BF16, name="grouped", align_bytes=64)
            grouped[n] = grouped_t
            for j in reversed(range(k)):
                nc.vector.tensor_tensor(
                    out=grouped_t[:, j].rearrange("p g r (u e) -> p (g r) u e", u=2),
                    in0=t1[n, j][:].rearrange("p u g r -> p (u g r)").bitcast(BF16).rearrange("p (u q e) -> p q u e", u=2, e=2),
                    in1=ascale_full[:].rearrange("p g r (u e) -> p (g r) u e", u=2),
                    op=ALU.mult,
                )

        def quant_attn(n, k):
            codes_t = work.tile([P, 4 * P], U32, name="codes", align_bytes=64)
            planes_t = work.tile([P, 4 * P], U8, name="planes", align_bytes=64)
            codes[n], planes[n] = codes_t, planes_t
            cols = slice(0, 2 * P * k)
            nc.vector.quantize_mx(out=codes_t[:, cols].bitcast(FP8X4), scales=planes_t[:, cols], in_=grouped[n][:, 0:k].rearrange("p j g r t -> p (j g r t)"))

        def project(n, k):
            for j in range(k):
                acc_t = ps2.tile([P, D], F32, name="acc")
                acc[n, j] = acc_t
                for g in range(2):
                    cols = slice((2 * j + g) * P, (2 * j + g + 1) * P)
                    nc.tensor.matmul_mx(
                        out=acc_t[:],
                        lhsT=codes[n][:, cols].bitcast(FP8X4),
                        lhsT_scale=planes[n][:, cols],
                        rhs=wo_t[:, 2 * D * g : 2 * D * (g + 1)].bitcast(FP4X4),
                        rhs_scale=wplanes[:, D * g : D * (g + 1)],
                        start=(g == 0),
                        stop=(g == 1),
                    )

        def add_bo(n, k):
            xb_t = work.tile([P, 2, D], F32, name="xb", bufs=3)
            xb[n] = xb_t
            for j in range(k):
                nc.gpsimd.tensor_tensor(out=xb_t[:, j, :], in0=xin[n][:, j, :], in1=bo_b[:], op=ALU.add)

        def residual(n, k):
            t = GROUPS[n][0]
            xm_t = deep.tile([P, 2, D], F32, name="xm")
            xm[n] = xm_t
            for j in reversed(range(k)):
                nc.vector.tensor_tensor(out=xm_t[:, j, :], in0=acc[n, j][:], in1=xb[n][:, j, :], op=ALU.add)
            nc.sync.dma_start(out=mid_v[:, t : t + k, :], in_=xm_t[:, 0:k, :])

        def squares(n, k):
            ss_t = work.tile([P, 2], F32, name="ss", bufs=4)
            for j in reversed(range(k)):
                junk = work.tile([P, D], BF16, name="junk")
                nc.scalar.activation(out=junk[:], in_=xm[n][:, j, :], func=ACT.Square, accum_out=ss_t[:, j : j + 1])
            ms_t = work.tile([P, 2], F32, name="ms", bufs=4)
            ms[n] = ms_t
            nc.scalar.activation(out=ms_t[:, 0:k], in_=ss_t[:, 0:k], func=ACT.Copy, scale=1.0 / D, bias=EPS)

        def root(n, k):
            rstd_t = work.tile([P, 2], F32, name="rstd", bufs=4)
            rstd[n] = rstd_t
            nc.gpsimd.tensor_tensor(out=rstd_t[:, 0:k], in0=ms[n][:, 0:k], in1=half[:, 0:k], op=ALU.pow)

        def norm(n, k):
            h_t = work.tile([P, 2, D], BF16, name="h")
            h[n] = h_t
            for j in reversed(range(k)):
                nc.vector.scalar_tensor_tensor(out=h_t[:, j, :], in0=xm[n][:, j, :], scalar=rstd[n][:, j : j + 1], in1=gain[:], op0=ALU.mult, op1=ALU.mult)

        def turn_h(n, k):
            bank = ps1.tile([P, 2, 2, P], F32, name="t2")
            t2[n] = bank
            for j in reversed(range(k)):
                words = h[n][:, j, :].bitcast(F32)
                for u in range(2):
                    nc.tensor.transpose(bank[:, j, u, :], words[:, u:256:2], ident[:])

        def group_h(n, k):
            h4_t = work.tile([P, 2, P, 4], BF16, name="h4", align_bytes=64)
            h4[n] = h4_t
            copy = nc.vector.tensor_copy if ("group_h", n) in ON_VECTOR else nc.scalar.copy
            copy(out=h4_t[:].rearrange("p j r t -> p (j r t)").bitcast(F32).rearrange("p (j r u) -> p j r u", j=2, u=2)[:, 0:k], in_=t2[n][:, 0:k].rearrange("p j u r -> p j r u"))

        def quant_h(n, k):
            hcodes_t = work.tile([P, 2 * P], U32, name="hcodes", align_bytes=64)
            hplanes_t = work.tile([P, 2 * P], U8, name="hplanes", align_bytes=64)
            hcodes[n], hplanes[n] = hcodes_t, hplanes_t
            nc.vector.quantize_mx(out=hcodes_t[:, 0 : P * k].bitcast(FP8X4), scales=hplanes_t[:, 0 : P * k], in_=h4[n][:, 0:k].rearrange("p j r t -> p (j r t)"))

        def expand(n, k):
            bank = ps1.tile([P, 2, 2 * P], F32, name="mx2")
            mx2[n] = bank
            for c in range(2):
                nc.tensor.matmul_mx(
                    out=bank[:, c, 0 : P * k],
                    lhsT=w1_t[:, 2 * P * c : 2 * P * (c + 1)].bitcast(FP4X4),
                    lhsT_scale=wplanes[:, 2 * D + P * c : 2 * D + P * (c + 1)],
                    rhs=hcodes[n][:, 0 : P * k].bitcast(FP8X4),
                    rhs_scale=hplanes[n][:, 0 : P * k],
                    start=True,
                    stop=True,
                )

        def gelu(n, k):
            gt_t = work.tile([P, 2, 2 * P], F32, name="gt")
            gt[n] = gt_t
            for c in range(2):
                nc.scalar.activation(out=gt_t[:, c, 0 : P * k], in_=mx2[n][:, c, 0 : P * k], func=ACT.Gelu, bias=b1_col[:, c : c + 1])

        def turn_g(n, k):
            bank = ps1.tile([P, 2, 2, P], F32, name="t3")
            t3[n] = bank
            for j in range(k):
                for c in range(2):
                    nc.tensor.transpose(bank[:, j, c, :], gt[n][:, c, P * j : P * (j + 1)], ident[:])

        def store_g(n, k):
            t = GROUPS[n][0]
            g_t = work.tile([P, 2, F], F32, name="g", bufs=3)
            copy = nc.vector.tensor_copy if ("store_g", n) in ON_VECTOR else nc.scalar.copy
            copy(out=g_t[:, 0:k, :], in_=t3[n][:, 0:k].rearrange("p j c r -> p j (c r)"))
            nc.sync.dma_start(out=g_v[:, t : t + k, :], in_=g_t[:, 0:k, :])

        stages = {
            "scale_attn": scale_attn,
            "residual": residual,
            "cast": cast,
            "gelu": gelu,
            "turn_h": turn_h,
            "turn_g": turn_g,
            "turn_attn": turn_attn,
            "group_h": group_h,
            "squares": squares,
            "add_bo": add_bo,
            "store_g": store_g,
            "root": root,
            "quant_h": quant_h,
            "quant_attn": quant_attn,
            "expand": expand,
            "project": project,
            "norm": norm,
        }
        warm_up()
        first_tile()
        cast(1, len(GROUPS[1]))
        early = {("cast", 0), ("cast", 1), ("turn_attn", 0), ("scale_attn", 0)}
        for step in range(len(GROUPS)):
            for name, lag in STEPS:
                n = step + lag
                if (name, n) == ("project", 0):
                    spread_bo()
                if 0 <= n < len(GROUPS) and (name, n) not in early:
                    stages[name](n, len(GROUPS[n]))
                if (name, n) == ("project", 1):
                    spread_gain_b1()
        for name, n in DRAIN:
            stages[name](n, len(GROUPS[n]))
